import numpy as np
import ml_dtypes


def mxq(x, axis, fmt="e4m3"):
    dtype, down = {"e4m3": (ml_dtypes.float8_e4m3fn, 7), "e5m2": (ml_dtypes.float8_e5m2, 14)}[fmt]
    v = np.moveaxis(np.asarray(x, np.float32).astype(ml_dtypes.bfloat16).astype(np.float64), axis, -1)
    blocks = v.reshape(v.shape[:-1] + (-1, 32))
    amax = np.abs(blocks).max(-1, keepdims=True)
    byte = np.maximum(np.where(amax > 0, np.frexp(amax)[1] - 1 + 127, 0) - down, 1)
    scale = np.exp2(byte - 127.0)
    codes = (blocks / scale).astype(np.float32).astype(dtype).astype(np.float64)
    return np.moveaxis((codes * scale).reshape(v.shape), -1, axis)


WIDE = False


def mx_kscale(k):
    if not WIDE:
        return np.ones(k)
    levels = np.array([10, -10, 5, -5, 0])
    a = np.random.permutation(np.resize(levels, k // 512 * 4)).reshape(k // 512, 4)
    idx = np.arange(k)
    return np.exp2(a[idx // 512, idx % 128 // 32])


BF16 = ml_dtypes.bfloat16


def bf(x):
    return np.asarray(x, np.float32).astype(BF16)


def f64(x):
    return np.asarray(x).astype(np.float64)


B, J, I, O = 4096, 3, 512, 256
IN_CH = J * I
OUT_CH = J * O
NEIGHBOUR_LIST = [[j for j in (i - 1, i, i + 1) if 0 <= j < J] for i in range(J)]


def build_mask():
    mask = np.zeros((OUT_CH, IN_CH))
    for i, neigh in enumerate(NEIGHBOUR_LIST):
        mask[i * O:(i + 1) * O, neigh[0] * I:(neigh[-1] + 1) * I] = 1.0
    return mask


def setup_inputs():
    s = mx_kscale(IN_CH)
    keep = np.random.random((OUT_CH, IN_CH)) < 0.75
    return {"x": bf(np.random.standard_normal((B, IN_CH)) * s),
            "weight": bf(np.random.standard_normal((OUT_CH, IN_CH)) / np.sqrt(0.75 * 3 * I) / s[None, :]),
            "mask": bf(build_mask() * keep),
            "bias": bf(np.random.standard_normal(OUT_CH) * 0.5)}


def reference(x, weight, mask, bias):
    x2 = f64(x).reshape(x.shape[0], -1)
    w = f64(weight) * f64(mask)
    xq = mxq(x2, 1, "e4m3")
    cols = []
    for i, neigh in enumerate(NEIGHBOUR_LIST):
        lo, hi = neigh[0] * I, (neigh[-1] + 1) * I
        cols.append(xq[:, lo:hi] @ mxq(w[i * O:(i + 1) * O, lo:hi], 1, "e4m3").T)
    return np.concatenate(cols, axis=1) + f64(bias)

@@ -1,0 +1,246 @@
+from contextlib import ExitStack
+
+import concourse.mybir as mybir
+from concourse.masks import make_identity
+
+F32 = mybir.dt.float32
+BF16 = mybir.dt.bfloat16
+U32 = mybir.dt.uint32
+U8 = mybir.dt.uint8
+FP8X4 = mybir.dt.float8_e4m3fn_x4
+ADD = mybir.AluOpType.add
+MULT = mybir.AluOpType.mult
+
+P = 128
+B, J, I, O = 4096, 3, 512, 256
+K = J * I
+N = J * O
+NEIGH = [[c for c in (j - 1, j, j + 1) if 0 <= c < J] for j in range(J)]
+N_CHUNKS = sum(len(n) for n in NEIGH)
+FLOPS = 2 * B * O * I * N_CHUNKS
+BYTES = 2 * B * K + 2 * 2 * O * I * N_CHUNKS + 2 * N + 4 * B * N
+
+MACROS = [2, 2, 2, 2, 4, 4, 4, 4, 4, 4]
+N_UNITS = B // (2 * P)
+LEAD = 6
+OUT_BUFS = 6
+
+
+def tile_skeletonlinear_t_kernel(tc, x, weight, mask, bias, out):
+    nc = tc.nc
+    first_unit = [sum(MACROS[:m]) // 2 for m in range(len(MACROS))]
+    unit_macro = []
+    for m, n in enumerate(MACROS):
+        for a in range(n // 2):
+            unit_macro.append((m, a))
+    assert len(unit_macro) == N_UNITS
+
+    with ExitStack() as ctx:
+        const = ctx.enter_context(tc.tile_pool(name="const", bufs=1))
+        ring = ctx.enter_context(tc.tile_pool(name="ring", bufs=3))
+        outs = ctx.enter_context(tc.tile_pool(name="outs", bufs=OUT_BUFS))
+        tps = ctx.enter_context(tc.psum_pool(name="tps", bufs=4))
+        ops = ctx.enter_context(tc.psum_pool(name="ops", bufs=4))
+        ctx.enter_context(tc.manual_schedule())
+
+        x_words = {}
+        state = {"next_macro": 0, "next_t": 0}
+        wt3 = {}
+        mk3 = {}
+        wm = {}
+        wg = {}
+        wc = {}
+        ws = {}
+        grp = {}
+        xc = {}
+        xs = {}
+        osb = {}
+
+        def load_x(m):
+            n = MACROS[m]
+            r0 = first_unit[m] * 2 * P
+            t = const.tile([P, n * K], BF16, name="x%d" % m)
+            nc.sync.dma_start(
+                out=t[:], in_=x[r0 : r0 + P * n, :].rearrange("(p t) k -> p (t k)", t=n)
+            )
+            x_words[m] = t[:].bitcast(F32)
+            state["next_macro"] = m + 1
+
+        def ensure_loads(unit):
+            while state["next_macro"] < len(MACROS) and first_unit[state["next_macro"]] <= unit:
+                load_x(state["next_macro"])
+
+        def load_w(j):
+            lo = NEIGH[j][0] * I
+            hi = (NEIGH[j][-1] + 1) * I
+            for views, src, nm in ((wt3, weight, "wt%d"), (mk3, mask, "mk%d")):
+                t = const.tile([P, 2 * (hi - lo)], BF16, name=nm % j)
+                view = t[:].rearrange("p (i k) -> p i k", i=2)
+                nc.sync.dma_start(
+                    out=view,
+                    in_=src[j * O : (j + 1) * O, lo:hi].rearrange("(i p) k -> p i k", p=P),
+                )
+                views[j] = view
+
+        def transposes4(words, cols):
+            bank = tps.tile([P, 4 * P], F32, name="tb", tag="tb")
+            for k, col in enumerate(cols):
+                nc.tensor.transpose(
+                    out=bank[:, k * P : (k + 1) * P],
+                    in_=words[:, col : col + P],
+                    identity=ident[:],
+                )
+            return bank
+
+        def regroup(bank, dst_words):
+            nc.scalar.copy(
+                out=dst_words.rearrange("p (q r h) -> p q r h", q=2, h=2),
+                in_=bank[:].rearrange("p (q h r) -> p q r h", q=2, h=2),
+            )
+
+        def w_joint(j):
+            for c in NEIGH[j]:
+                cl = c - NEIGH[j][0]
+                t = ring.tile([P, 2 * I], BF16, name="wm", tag="wm")
+                nc.vector.tensor_tensor(
+                    out=t[:].rearrange("p (i k) -> p i k", i=2),
+                    in0=wt3[j][:, :, cl * I : (cl + 1) * I],
+                    in1=mk3[j][:, :, cl * I : (cl + 1) * I],
+                    op=MULT,
+                )
+                wm[(j, c)] = t
+            for c in NEIGH[j]:
+                bank = transposes4(wm[(j, c)][:].bitcast(F32), [0, P, 2 * P, 3 * P])
+                g = ring.tile([P, 4 * O], BF16, name="wg", tag="wg", align_bytes=64)
+                regroup(bank, g[:].bitcast(F32))
+                wg[(j, c)] = g
+            for c in NEIGH[j]:
+                codes = const.tile([P, O], U32, name="wc%d%d" % (j, c), align_bytes=64)
+                scales = const.tile([P, O], U8, name="ws%d%d" % (j, c), align_bytes=64)
+                nc.vector.quantize_mx(
+                    out=codes[:].bitcast(FP8X4), scales=scales[:], in_=wg[(j, c)][:]
+                )
+                wc[(j, c)] = codes
+                ws[(j, c)] = scales
+
+        def t_unit(u):
+            m, a = unit_macro[u]
+            g_tile = ring.tile([P, 2 * K], BF16, name="grp", tag="grp", align_bytes=64)
+            grp[u] = g_tile
+            gw = g_tile[:].bitcast(F32)
+            base = a * K
+            for g in range(J):
+                cols = [base + t * (K // 2) + g * (I // 2) + h * P for t in range(2) for h in range(2)]
+                bank = transposes4(x_words[m], cols)
+                regroup(bank, gw[:, g * 4 * P : (g + 1) * 4 * P])
+            state["next_t"] = u + 1
+
+        def q_unit(u, g):
+            if g == 0:
+                xc[u] = ring.tile([P, 2 * J * P], U32, name="xc", tag="xc", align_bytes=64)
+                xs[u] = ring.tile([P, 2 * J * P], U8, name="xs", tag="xs", align_bytes=64)
+            nc.vector.quantize_mx(
+                out=xc[u][:, g * 2 * P : (g + 1) * 2 * P].bitcast(FP8X4),
+                scales=xs[u][:, g * 2 * P : (g + 1) * 2 * P],
+                in_=grp[u][:, g * 8 * P : (g + 1) * 8 * P],
+            )
+
+        def g_unit(u, j):
+            bank = ops.tile([P, 2 * O], F32, name="ob", tag="ob")
+            for t in range(2):
+                for c in NEIGH[j]:
+                    s = (2 * c + t) * P
+                    nc.tensor.matmul_mx(
+                        out=bank[:, t * O : (t + 1) * O],
+                        lhsT=xc[u][:, s : s + P].bitcast(FP8X4),
+                        lhsT_scale=xs[u][:, s : s + P],
+                        rhs=wc[(j, c)][:].bitcast(FP8X4),
+                        rhs_scale=ws[(j, c)][:],
+                        start=(c == NEIGH[j][0]),
+                        stop=(c == NEIGH[j][-1]),
+                    )
+            return bank
+
+        def a_unit(u, j, bank):
+            if u not in osb:
+                osb[u] = outs.tile([P, 2 * N], F32, name="osb", tag="osb")
+            nc.vector.tensor_tensor(
+                out=osb[u][:].rearrange("p (t o) -> p t o", t=2)[:, :, j * O : (j + 1) * O],
+                in0=bank[:].rearrange("p (t o) -> p t o", t=2),
+                in1=bias_sb[:, j * O : (j + 1) * O].unsqueeze(1).to_broadcast([P, 2, O]),
+                op=ADD,
+            )
+
+        def store(u, lo=0, hi=N):
+            m, a = unit_macro[u]
+            n = MACROS[m]
+            r0 = first_unit[m] * 2 * P
+            dram = out[r0 : r0 + P * n, :].rearrange("(p t) o -> p t o", t=n)
+            nc.sync.dma_start(
+                out=dram[:, 2 * a : 2 * a + 2, lo:hi],
+                in_=osb[u][:].rearrange("p (t o) -> p t o", t=2)[:, :, lo:hi],
+            )
+
+        brow = const.tile([P, N], BF16, name="brow")
+        ones = const.tile([P, P], BF16, name="ones")
+        ident = const.tile([P, P], F32, name="ident")
+        bias_sb = const.tile([P, N], F32, name="bias_sb")
+        nc.vector.memset(brow[:], 0.0)
+        nc.vector.memset(ones[:], 1.0)
+        make_identity(nc, ident[:])
+        nc.scalar.dma_start(out=brow[0:1, :], in_=bias.rearrange("(o n) -> o n", o=1))
+
+        load_w(0)
+        load_x(0)
+        load_w(1)
+        load_x(1)
+        load_w(2)
+        ensure_loads(LEAD)
+
+        for lo, hi in ((0, 512), (512, N)):
+            bank = ops.tile([P, 2 * O], F32, name="ob", tag="ob")
+            nc.tensor.matmul(
+                out=bank[:, 0 : hi - lo], lhsT=ones[:], rhs=brow[:, lo:hi], start=True, stop=True
+            )
+            nc.scalar.copy(out=bias_sb[:, lo:hi], in_=bank[:, 0 : hi - lo])
+
+        w_joint(0)
+        t_unit(0)
+        for g in range(J):
+            q_unit(0, g)
+        a_unit(0, 0, g_unit(0, 0))
+        w_joint(1)
+        t_unit(1)
+        for g in range(J):
+            q_unit(1, g)
+        a_unit(0, 1, g_unit(0, 1))
+        a_unit(1, 0, g_unit(1, 0))
+        a_unit(1, 1, g_unit(1, 1))
+        w_joint(2)
+        t_unit(2)
+        bank = g_unit(0, 2)
+        q_unit(2, 0)
+        a_unit(0, 2, bank)
+        store(0)
+        bank = g_unit(1, 2)
+        q_unit(2, 1)
+        a_unit(1, 2, bank)
+        q_unit(2, 2)
+        store(1)
+
+        for i in range(2, N_UNITS):
+            lead = 1 if i < 4 else 2
+            while state["next_t"] < N_UNITS and state["next_t"] <= i + lead:
+                t_unit(state["next_t"])
+            for j in range(J):
+                bank = g_unit(i, j)
+                if i + 1 < N_UNITS:
+                    q_unit(i + 1, j)
+                a_unit(i, j, bank)
+                if i == N_UNITS - 1 and j == 1:
+                    store(i, 0, 2 * O)
+            ensure_loads(i + LEAD)
+            if i == N_UNITS - 1:
+                store(i, 2 * O, N)
+            else:
+                store(i)

@@ -20,10 +20,11 @@ N_CHUNKS = sum(len(n) for n in NEIGH)
 FLOPS = 2 * B * O * I * N_CHUNKS
 BYTES = 2 * B * K + 2 * 2 * O * I * N_CHUNKS + 2 * N + 4 * B * N
 
-MACROS = [2, 2, 2, 2, 4, 4, 4, 4, 4, 4]
+MACROS = [2, 2, 2, 2, 2, 2, 4, 4, 4, 4, 4]
 N_UNITS = B // (2 * P)
-LEAD = 6
-OUT_BUFS = 6
+OUT_BUFS = 10
+LEAD2_FROM = 6
+RELIEF = False
 
 
 def tile_skeletonlinear_t_kernel(tc, x, weight, mask, bias, out):
@@ -44,7 +45,7 @@ def tile_skeletonlinear_t_kernel(tc, x, weight, mask, bias, out):
         ctx.enter_context(tc.manual_schedule())
 
         x_words = {}
-        state = {"next_macro": 0, "next_t": 0}
+        state = {"next_t": 0}
         wt3 = {}
         mk3 = {}
         wm = {}
@@ -64,17 +65,12 @@ def tile_skeletonlinear_t_kernel(tc, x, weight, mask, bias, out):
                 out=t[:], in_=x[r0 : r0 + P * n, :].rearrange("(p t) k -> p (t k)", t=n)
             )
             x_words[m] = t[:].bitcast(F32)
-            state["next_macro"] = m + 1
-
-        def ensure_loads(unit):
-            while state["next_macro"] < len(MACROS) and first_unit[state["next_macro"]] <= unit:
-                load_x(state["next_macro"])
 
         def load_w(j):
             lo = NEIGH[j][0] * I
             hi = (NEIGH[j][-1] + 1) * I
             for views, src, nm in ((wt3, weight, "wt%d"), (mk3, mask, "mk%d")):
-                t = const.tile([P, 2 * (hi - lo)], BF16, name=nm % j)
+                t = outs.tile([P, 2 * (hi - lo)], BF16, name=nm % j, tag="osb")
                 view = t[:].rearrange("p (i k) -> p i k", i=2)
                 nc.sync.dma_start(
                     out=view,
@@ -135,15 +131,15 @@ def tile_skeletonlinear_t_kernel(tc, x, weight, mask, bias, out):
                 regroup(bank, gw[:, g * 4 * P : (g + 1) * 4 * P])
             state["next_t"] = u + 1
 
-        def q_unit(u, g):
-            if g == 0:
-                xc[u] = ring.tile([P, 2 * J * P], U32, name="xc", tag="xc", align_bytes=64)
-                xs[u] = ring.tile([P, 2 * J * P], U8, name="xs", tag="xs", align_bytes=64)
-            nc.vector.quantize_mx(
-                out=xc[u][:, g * 2 * P : (g + 1) * 2 * P].bitcast(FP8X4),
-                scales=xs[u][:, g * 2 * P : (g + 1) * 2 * P],
-                in_=grp[u][:, g * 8 * P : (g + 1) * 8 * P],
-            )
+        def q_unit(u):
+            xc[u] = ring.tile([P, 2 * J * P], U32, name="xc", tag="xc", align_bytes=64)
+            xs[u] = ring.tile([P, 2 * J * P], U8, name="xs", tag="xs", align_bytes=64)
+            for lo, hi in ((0, 4 * P), (4 * P, 6 * P)):
+                nc.vector.quantize_mx(
+                    out=xc[u][:, lo:hi].bitcast(FP8X4),
+                    scales=xs[u][:, lo:hi],
+                    in_=grp[u][:, 4 * lo : 4 * hi],
+                )
 
         def g_unit(u, j):
             bank = ops.tile([P, 2 * O], F32, name="ob", tag="ob")
@@ -161,15 +157,17 @@ def tile_skeletonlinear_t_kernel(tc, x, weight, mask, bias, out):
                     )
             return bank
 
-        def a_unit(u, j, bank):
+        def a_unit(u, j, bank, relief=False):
             if u not in osb:
                 osb[u] = outs.tile([P, 2 * N], F32, name="osb", tag="osb")
-            nc.vector.tensor_tensor(
-                out=osb[u][:].rearrange("p (t o) -> p t o", t=2)[:, :, j * O : (j + 1) * O],
-                in0=bank[:].rearrange("p (t o) -> p t o", t=2),
-                in1=bias_sb[:, j * O : (j + 1) * O].unsqueeze(1).to_broadcast([P, 2, O]),
-                op=ADD,
-            )
+            dst = osb[u][:].rearrange("p (t o) -> p t o", t=2)[:, :, j * O : (j + 1) * O]
+            acc = bank[:].rearrange("p (t o) -> p t o", t=2)
+            bias_j = bias_sb[:, j * O : (j + 1) * O].unsqueeze(1).to_broadcast([P, 2, O])
+            if relief:
+                nc.scalar.copy(out=dst, in_=acc)
+                nc.gpsimd.tensor_tensor(out=dst, in0=dst, in1=bias_j, op=ADD)
+            else:
+                nc.vector.tensor_tensor(out=dst, in0=acc, in1=bias_j, op=ADD)
 
         def store(u, lo=0, hi=N):
             m, a = unit_macro[u]
@@ -188,59 +186,52 @@ def tile_skeletonlinear_t_kernel(tc, x, weight, mask, bias, out):
         nc.vector.memset(brow[:], 0.0)
         nc.vector.memset(ones[:], 1.0)
         make_identity(nc, ident[:])
-        nc.scalar.dma_start(out=brow[0:1, :], in_=bias.rearrange("(o n) -> o n", o=1))
 
         load_w(0)
         load_x(0)
+        nc.sync.dma_start(out=brow[0:1, :], in_=bias.rearrange("(o n) -> o n", o=1))
         load_w(1)
         load_x(1)
         load_w(2)
-        ensure_loads(LEAD)
+        for m in range(2, len(MACROS)):
+            load_x(m)
 
+        w_joint(0)
+        t_unit(0)
         for lo, hi in ((0, 512), (512, N)):
             bank = ops.tile([P, 2 * O], F32, name="ob", tag="ob")
             nc.tensor.matmul(
                 out=bank[:, 0 : hi - lo], lhsT=ones[:], rhs=brow[:, lo:hi], start=True, stop=True
             )
             nc.scalar.copy(out=bias_sb[:, lo:hi], in_=bank[:, 0 : hi - lo])
-
-        w_joint(0)
-        t_unit(0)
-        for g in range(J):
-            q_unit(0, g)
+        q_unit(0)
         a_unit(0, 0, g_unit(0, 0))
         w_joint(1)
         t_unit(1)
-        for g in range(J):
-            q_unit(1, g)
+        q_unit(1)
         a_unit(0, 1, g_unit(0, 1))
         a_unit(1, 0, g_unit(1, 0))
         a_unit(1, 1, g_unit(1, 1))
         w_joint(2)
         t_unit(2)
-        bank = g_unit(0, 2)
-        q_unit(2, 0)
-        a_unit(0, 2, bank)
+        q_unit(2)
+        a_unit(0, 2, g_unit(0, 2))
         store(0)
-        bank = g_unit(1, 2)
-        q_unit(2, 1)
-        a_unit(1, 2, bank)
-        q_unit(2, 2)
+        a_unit(1, 2, g_unit(1, 2))
         store(1)
 
         for i in range(2, N_UNITS):
-            lead = 1 if i < 4 else 2
+            last = i == N_UNITS - 1
+            lead = 1 if i < LEAD2_FROM else 2
             while state["next_t"] < N_UNITS and state["next_t"] <= i + lead:
                 t_unit(state["next_t"])
+            if not last:
+                q_unit(i + 1)
             for j in range(J):
-                bank = g_unit(i, j)
-                if i + 1 < N_UNITS:
-                    q_unit(i + 1, j)
-                a_unit(i, j, bank)
-                if i == N_UNITS - 1 and j == 1:
+                a_unit(i, j, g_unit(i, j), relief=(RELIEF and j == 0))
+                if last and j == 1:
                     store(i, 0, 2 * O)
-            ensure_loads(i + LEAD)
-            if i == N_UNITS - 1:
+            if last:
                 store(i, 2 * O, N)
             else:
                 store(i)

@@ -20,10 +20,11 @@ N_CHUNKS = sum(len(n) for n in NEIGH)
 FLOPS = 2 * B * O * I * N_CHUNKS
 BYTES = 2 * B * K + 2 * 2 * O * I * N_CHUNKS + 2 * N + 4 * B * N
 
-MACROS = [2, 2, 2, 2, 2, 2, 4, 4, 4, 4, 4]
+MACROS = [2, 2, 2, 2, 2, 2, 2, 2, 4, 4, 4, 4]
 N_UNITS = B // (2 * P)
 OUT_BUFS = 10
 LEAD2_FROM = 6
+ROUNDS = [((3, 4), (2,))] + [((a + 2, a + 3), (a, a + 1)) for a in range(3, 13, 2)] + [((15,), (13, 14)), ((), (15,))]
 RELIEF = False
 
 
@@ -220,18 +221,20 @@ def tile_skeletonlinear_t_kernel(tc, x, weight, mask, bias, out):
         a_unit(1, 2, g_unit(1, 2))
         store(1)
 
-        for i in range(2, N_UNITS):
-            last = i == N_UNITS - 1
-            lead = 1 if i < LEAD2_FROM else 2
-            while state["next_t"] < N_UNITS and state["next_t"] <= i + lead:
-                t_unit(state["next_t"])
-            if not last:
-                q_unit(i + 1)
-            for j in range(J):
-                a_unit(i, j, g_unit(i, j), relief=(RELIEF and j == 0))
-                if last and j == 1:
-                    store(i, 0, 2 * O)
-            if last:
-                store(i, 2 * O, N)
-            else:
-                store(i)
+        for t_run, g_run in ROUNDS:
+            for u in t_run:
+                t_unit(u)
+            for n, i in enumerate(g_run):
+                last = i == N_UNITS - 1
+                if n < len(t_run):
+                    q_unit(t_run[n])
+                for j in range(J):
+                    a_unit(i, j, g_unit(i, j), relief=(RELIEF and j == 0))
+                    if last and j == 1:
+                        store(i, 0, 2 * O)
+                if last:
+                    store(i, 2 * O, N)
+                else:
+                    store(i)
+            for u in t_run[len(g_run) :]:
+                q_unit(u)

@@ -20,11 +20,10 @@ N_CHUNKS = sum(len(n) for n in NEIGH)
 FLOPS = 2 * B * O * I * N_CHUNKS
 BYTES = 2 * B * K + 2 * 2 * O * I * N_CHUNKS + 2 * N + 4 * B * N
 
-MACROS = [2, 2, 2, 2, 2, 2, 2, 2, 4, 4, 4, 4]
+MACROS = [2, 2, 2, 2, 2, 2, 4, 4, 4, 4, 4]
 N_UNITS = B // (2 * P)
 OUT_BUFS = 10
 LEAD2_FROM = 6
-ROUNDS = [((3, 4), (2,))] + [((a + 2, a + 3), (a, a + 1)) for a in range(3, 13, 2)] + [((15,), (13, 14)), ((), (15,))]
 RELIEF = False
 
 
@@ -95,7 +94,7 @@ def tile_skeletonlinear_t_kernel(tc, x, weight, mask, bias, out):
                 in_=bank[:].rearrange("p (q h r) -> p q r h", q=2, h=2),
             )
 
-        def w_joint(j):
+        def w_mult(j):
             for c in NEIGH[j]:
                 cl = c - NEIGH[j][0]
                 t = ring.tile([P, 2 * I], BF16, name="wm", tag="wm")
@@ -106,11 +105,15 @@ def tile_skeletonlinear_t_kernel(tc, x, weight, mask, bias, out):
                     op=MULT,
                 )
                 wm[(j, c)] = t
+
+        def w_tr(j):
             for c in NEIGH[j]:
                 bank = transposes4(wm[(j, c)][:].bitcast(F32), [0, P, 2 * P, 3 * P])
                 g = ring.tile([P, 4 * O], BF16, name="wg", tag="wg", align_bytes=64)
                 regroup(bank, g[:].bitcast(F32))
                 wg[(j, c)] = g
+
+        def w_q(j):
             for c in NEIGH[j]:
                 codes = const.tile([P, O], U32, name="wc%d%d" % (j, c), align_bytes=64)
                 scales = const.tile([P, O], U8, name="ws%d%d" % (j, c), align_bytes=64)
@@ -197,44 +200,58 @@ def tile_skeletonlinear_t_kernel(tc, x, weight, mask, bias, out):
         for m in range(2, len(MACROS)):
             load_x(m)
 
-        w_joint(0)
+        def bias_to_all_partitions():
+            for lo, hi in ((0, 512), (512, N)):
+                bank = ops.tile([P, 2 * O], F32, name="ob", tag="ob")
+                nc.tensor.matmul(
+                    out=bank[:, 0 : hi - lo], lhsT=ones[:], rhs=brow[:, lo:hi], start=True, stop=True
+                )
+                nc.scalar.copy(out=bias_sb[:, lo:hi], in_=bank[:, 0 : hi - lo])
+
+        acc = {}
+        w_mult(0)
+        w_tr(0)
         t_unit(0)
-        for lo, hi in ((0, 512), (512, N)):
-            bank = ops.tile([P, 2 * O], F32, name="ob", tag="ob")
-            nc.tensor.matmul(
-                out=bank[:, 0 : hi - lo], lhsT=ones[:], rhs=brow[:, lo:hi], start=True, stop=True
-            )
-            nc.scalar.copy(out=bias_sb[:, lo:hi], in_=bank[:, 0 : hi - lo])
+        bias_to_all_partitions()
+        w_q(0)
         q_unit(0)
-        a_unit(0, 0, g_unit(0, 0))
-        w_joint(1)
+        acc[(0, 0)] = g_unit(0, 0)
+        w_mult(1)
+        w_tr(1)
         t_unit(1)
+        a_unit(0, 0, acc[(0, 0)])
+        w_q(1)
+        acc[(0, 1)] = g_unit(0, 1)
+        w_mult(2)
+        w_tr(2)
         q_unit(1)
-        a_unit(0, 1, g_unit(0, 1))
-        a_unit(1, 0, g_unit(1, 0))
-        a_unit(1, 1, g_unit(1, 1))
-        w_joint(2)
         t_unit(2)
+        acc[(1, 0)] = g_unit(1, 0)
+        acc[(1, 1)] = g_unit(1, 1)
+        a_unit(0, 1, acc[(0, 1)])
+        w_q(2)
+        a_unit(1, 0, acc[(1, 0)])
+        acc[(0, 2)] = g_unit(0, 2)
+        acc[(1, 2)] = g_unit(1, 2)
+        a_unit(1, 1, acc[(1, 1)])
         q_unit(2)
-        a_unit(0, 2, g_unit(0, 2))
+        a_unit(0, 2, acc[(0, 2)])
         store(0)
-        a_unit(1, 2, g_unit(1, 2))
+        a_unit(1, 2, acc[(1, 2)])
         store(1)
 
-        for t_run, g_run in ROUNDS:
-            for u in t_run:
-                t_unit(u)
-            for n, i in enumerate(g_run):
-                last = i == N_UNITS - 1
-                if n < len(t_run):
-                    q_unit(t_run[n])
-                for j in range(J):
-                    a_unit(i, j, g_unit(i, j), relief=(RELIEF and j == 0))
-                    if last and j == 1:
-                        store(i, 0, 2 * O)
-                if last:
-                    store(i, 2 * O, N)
-                else:
-                    store(i)
-            for u in t_run[len(g_run) :]:
-                q_unit(u)
+        for i in range(2, N_UNITS):
+            last = i == N_UNITS - 1
+            lead = 1 if i < LEAD2_FROM else 2
+            while state["next_t"] < N_UNITS and state["next_t"] <= i + lead:
+                t_unit(state["next_t"])
+            if not last:
+                q_unit(i + 1)
+            for j in range(J):
+                a_unit(i, j, g_unit(i, j), relief=(RELIEF and j == 0))
+                if last and j == 1:
+                    store(i, 0, 2 * O)
+            if last:
+                store(i, 2 * O, N)
+            else:
+                store(i)

@@ -23,8 +23,8 @@ BYTES = 2 * B * K + 2 * 2 * O * I * N_CHUNKS + 2 * N + 4 * B * N
 MACROS = [2, 2, 2, 2, 2, 2, 4, 4, 4, 4, 4]
 N_UNITS = B // (2 * P)
 OUT_BUFS = 10
-LEAD2_FROM = 6
-RELIEF = False
+LONGER_RUNS = (3, 4, 5)
+SPLIT_LAST = 2
 
 
 def tile_skeletonlinear_t_kernel(tc, x, weight, mask, bias, out):
@@ -45,7 +45,6 @@ def tile_skeletonlinear_t_kernel(tc, x, weight, mask, bias, out):
         ctx.enter_context(tc.manual_schedule())
 
         x_words = {}
-        state = {"next_t": 0}
         wt3 = {}
         mk3 = {}
         wm = {}
@@ -123,17 +122,17 @@ def tile_skeletonlinear_t_kernel(tc, x, weight, mask, bias, out):
                 wc[(j, c)] = codes
                 ws[(j, c)] = scales
 
-        def t_unit(u):
+        def t_bank(u, g):
             m, a = unit_macro[u]
-            g_tile = ring.tile([P, 2 * K], BF16, name="grp", tag="grp", align_bytes=64)
-            grp[u] = g_tile
-            gw = g_tile[:].bitcast(F32)
-            base = a * K
+            if g == 0:
+                grp[u] = ring.tile([P, 2 * K], BF16, name="grp", tag="grp", align_bytes=64)
+            cols = [a * K + t * (K // 2) + g * (I // 2) + h * P for t in range(2) for h in range(2)]
+            bank = transposes4(x_words[m], cols)
+            regroup(bank, grp[u][:].bitcast(F32)[:, g * 4 * P : (g + 1) * 4 * P])
+
+        def t_unit(u):
             for g in range(J):
-                cols = [base + t * (K // 2) + g * (I // 2) + h * P for t in range(2) for h in range(2)]
-                bank = transposes4(x_words[m], cols)
-                regroup(bank, gw[:, g * 4 * P : (g + 1) * 4 * P])
-            state["next_t"] = u + 1
+                t_bank(u, g)
 
         def q_unit(u):
             xc[u] = ring.tile([P, 2 * J * P], U32, name="xc", tag="xc", align_bytes=64)
@@ -240,18 +239,18 @@ def tile_skeletonlinear_t_kernel(tc, x, weight, mask, bias, out):
         a_unit(1, 2, acc[(1, 2)])
         store(1)
 
+        t_banks = [(u, g) for u in range(3, N_UNITS) for g in range(J)]
+        done = 0
         for i in range(2, N_UNITS):
-            last = i == N_UNITS - 1
-            lead = 1 if i < LEAD2_FROM else 2
-            while state["next_t"] < N_UNITS and state["next_t"] <= i + lead:
-                t_unit(state["next_t"])
-            if not last:
+            n = J + (1 if i in LONGER_RUNS else 0)
+            for u, g in t_banks[done : done + n]:
+                t_bank(u, g)
+            done += n
+            if i + 1 < N_UNITS:
                 q_unit(i + 1)
             for j in range(J):
-                a_unit(i, j, g_unit(i, j), relief=(RELIEF and j == 0))
-                if last and j == 1:
-                    store(i, 0, 2 * O)
-            if last:
-                store(i, 2 * O, N)
-            else:
+                a_unit(i, j, g_unit(i, j))
+                if i >= N_UNITS - SPLIT_LAST:
+                    store(i, j * O, (j + 1) * O)
+            if i < N_UNITS - SPLIT_LAST:
                 store(i)

@@ -23,6 +23,7 @@ BYTES = 2 * B * K + 2 * 2 * O * I * N_CHUNKS + 2 * N + 4 * B * N
 MACROS = [2, 2, 2, 2, 2, 2, 4, 4, 4, 4, 4]
 N_UNITS = B // (2 * P)
 OUT_BUFS = 10
+XB = 3
 LONGER_RUNS = (3, 4, 5)
 SPLIT_LAST = 2
 
@@ -39,6 +40,7 @@ def tile_skeletonlinear_t_kernel(tc, x, weight, mask, bias, out):
     with ExitStack() as ctx:
         const = ctx.enter_context(tc.tile_pool(name="const", bufs=1))
         ring = ctx.enter_context(tc.tile_pool(name="ring", bufs=3))
+        xring = ctx.enter_context(tc.tile_pool(name="xring", bufs=XB))
         outs = ctx.enter_context(tc.tile_pool(name="outs", bufs=OUT_BUFS))
         tps = ctx.enter_context(tc.psum_pool(name="tps", bufs=4))
         ops = ctx.enter_context(tc.psum_pool(name="ops", bufs=4))
@@ -93,8 +95,8 @@ def tile_skeletonlinear_t_kernel(tc, x, weight, mask, bias, out):
                 in_=bank[:].rearrange("p (q h r) -> p q r h", q=2, h=2),
             )
 
-        def w_mult(j):
-            for c in NEIGH[j]:
+        def w_mult(j, cs=None):
+            for c in cs or NEIGH[j]:
                 cl = c - NEIGH[j][0]
                 t = ring.tile([P, 2 * I], BF16, name="wm", tag="wm")
                 nc.vector.tensor_tensor(
@@ -105,15 +107,15 @@ def tile_skeletonlinear_t_kernel(tc, x, weight, mask, bias, out):
                 )
                 wm[(j, c)] = t
 
-        def w_tr(j):
-            for c in NEIGH[j]:
+        def w_tr(j, cs=None):
+            for c in cs or NEIGH[j]:
                 bank = transposes4(wm[(j, c)][:].bitcast(F32), [0, P, 2 * P, 3 * P])
                 g = ring.tile([P, 4 * O], BF16, name="wg", tag="wg", align_bytes=64)
                 regroup(bank, g[:].bitcast(F32))
                 wg[(j, c)] = g
 
-        def w_q(j):
-            for c in NEIGH[j]:
+        def w_q(j, cs=None):
+            for c in cs or NEIGH[j]:
                 codes = const.tile([P, O], U32, name="wc%d%d" % (j, c), align_bytes=64)
                 scales = const.tile([P, O], U8, name="ws%d%d" % (j, c), align_bytes=64)
                 nc.vector.quantize_mx(
@@ -125,7 +127,7 @@ def tile_skeletonlinear_t_kernel(tc, x, weight, mask, bias, out):
         def t_bank(u, g):
             m, a = unit_macro[u]
             if g == 0:
-                grp[u] = ring.tile([P, 2 * K], BF16, name="grp", tag="grp", align_bytes=64)
+                grp[u] = xring.tile([P, 2 * K], BF16, name="grp", tag="grp", align_bytes=64)
             cols = [a * K + t * (K // 2) + g * (I // 2) + h * P for t in range(2) for h in range(2)]
             bank = transposes4(x_words[m], cols)
             regroup(bank, grp[u][:].bitcast(F32)[:, g * 4 * P : (g + 1) * 4 * P])
@@ -135,8 +137,8 @@ def tile_skeletonlinear_t_kernel(tc, x, weight, mask, bias, out):
                 t_bank(u, g)
 
         def q_unit(u):
-            xc[u] = ring.tile([P, 2 * J * P], U32, name="xc", tag="xc", align_bytes=64)
-            xs[u] = ring.tile([P, 2 * J * P], U8, name="xs", tag="xs", align_bytes=64)
+            xc[u] = xring.tile([P, 2 * J * P], U32, name="xc", tag="xc", align_bytes=64)
+            xs[u] = xring.tile([P, 2 * J * P], U8, name="xs", tag="xs", align_bytes=64)
             for lo, hi in ((0, 4 * P), (4 * P, 6 * P)):
                 nc.vector.quantize_mx(
                     out=xc[u][:, lo:hi].bitcast(FP8X4),
@@ -182,6 +184,13 @@ def tile_skeletonlinear_t_kernel(tc, x, weight, mask, bias, out):
                 in_=osb[u][:].rearrange("p (t o) -> p t o", t=2)[:, :, lo:hi],
             )
 
+        def keep_warm(n):
+            bank = ops.tile([P, 2 * O], F32, name="ob", tag="ob")
+            for r in range(n):
+                nc.tensor.matmul(out=bank[:], lhsT=filler[:, 0:P], rhs=filler[:], start=True, stop=True)
+
+        filler = const.tile([P, 2 * O], BF16, name="filler")
+        nc.vector.memset(filler[:], 0.0)
         brow = const.tile([P, N], BF16, name="brow")
         ones = const.tile([P, P], BF16, name="ones")
         ident = const.tile([P, P], F32, name="ident")
@@ -208,18 +217,22 @@ def tile_skeletonlinear_t_kernel(tc, x, weight, mask, bias, out):
                 nc.scalar.copy(out=bias_sb[:, lo:hi], in_=bank[:, 0 : hi - lo])
 
         acc = {}
+        keep_warm(11)
         w_mult(0)
         w_tr(0)
         t_unit(0)
         bias_to_all_partitions()
+        keep_warm(2)
         w_q(0)
         q_unit(0)
         acc[(0, 0)] = g_unit(0, 0)
+        keep_warm(3)
         w_mult(1)
         w_tr(1)
         t_unit(1)
         a_unit(0, 0, acc[(0, 0)])
         w_q(1)
+        keep_warm(2)
         acc[(0, 1)] = g_unit(0, 1)
         w_mult(2)
         w_tr(2)

@@ -24,8 +24,6 @@ MACROS = [2, 2, 2, 2, 2, 2, 4, 4, 4, 4, 4]
 N_UNITS = B // (2 * P)
 OUT_BUFS = 10
 XB = 3
-LONGER_RUNS = (3, 4, 5)
-SPLIT_LAST = 2
 
 
 def tile_skeletonlinear_t_kernel(tc, x, weight, mask, bias, out):
@@ -162,32 +160,49 @@ def tile_skeletonlinear_t_kernel(tc, x, weight, mask, bias, out):
                     )
             return bank
 
-        def a_unit(u, j, bank, relief=False):
+        def a_unit(u, j, bank):
             if u not in osb:
                 osb[u] = outs.tile([P, 2 * N], F32, name="osb", tag="osb")
             dst = osb[u][:].rearrange("p (t o) -> p t o", t=2)[:, :, j * O : (j + 1) * O]
             acc = bank[:].rearrange("p (t o) -> p t o", t=2)
             bias_j = bias_sb[:, j * O : (j + 1) * O].unsqueeze(1).to_broadcast([P, 2, O])
-            if relief:
-                nc.scalar.copy(out=dst, in_=acc)
-                nc.gpsimd.tensor_tensor(out=dst, in0=dst, in1=bias_j, op=ADD)
-            else:
-                nc.vector.tensor_tensor(out=dst, in0=acc, in1=bias_j, op=ADD)
+            nc.vector.tensor_tensor(out=dst, in0=acc, in1=bias_j, op=ADD)
 
-        def store(u, lo=0, hi=N):
+        def store(u, t0=0, n_rows=2):
             m, a = unit_macro[u]
             n = MACROS[m]
             r0 = first_unit[m] * 2 * P
             dram = out[r0 : r0 + P * n, :].rearrange("(p t) o -> p t o", t=n)
             nc.sync.dma_start(
-                out=dram[:, 2 * a : 2 * a + 2, lo:hi],
-                in_=osb[u][:].rearrange("p (t o) -> p t o", t=2)[:, :, lo:hi],
+                out=dram[:, 2 * a + t0 : 2 * a + t0 + n_rows, :],
+                in_=osb[u][:].rearrange("p (t o) -> p t o", t=2)[:, t0 : t0 + n_rows, :],
             )
 
         def keep_warm(n):
             bank = ops.tile([P, 2 * O], F32, name="ob", tag="ob")
             for r in range(n):
                 nc.tensor.matmul(out=bank[:], lhsT=filler[:, 0:P], rhs=filler[:], start=True, stop=True)
+
+        def row_tile(u, t, js):
+            if u not in osb:
+                osb[u] = outs.tile([P, 2 * N], F32, name="osb", tag="osb")
+            bank = ops.tile([P, 2 * O], F32, name="ob", tag="ob")
+            for k, j in enumerate(js):
+                for c in NEIGH[j]:
+                    s = (2 * c + t) * P
+                    nc.tensor.matmul_mx(
+                        out=bank[:, k * O : (k + 1) * O],
+                        lhsT=xc[u][:, s : s + P].bitcast(FP8X4),
+                        lhsT_scale=xs[u][:, s : s + P],
+                        rhs=wc[(j, c)][:].bitcast(FP8X4),
+                        rhs_scale=ws[(j, c)][:],
+                        start=(c == NEIGH[j][0]),
+                        stop=(c == NEIGH[j][-1]),
+                    )
+            lo, hi = js[0] * O, (js[-1] + 1) * O
+            nc.vector.tensor_tensor(
+                out=osb[u][:, t * N + lo : t * N + hi], in0=bank[:, 0 : hi - lo], in1=bias_sb[:, lo:hi], op=ADD
+            )
 
         filler = const.tile([P, 2 * O], BF16, name="filler")
         nc.vector.memset(filler[:], 0.0)
@@ -229,10 +244,10 @@ def tile_skeletonlinear_t_kernel(tc, x, weight, mask, bias, out):
         keep_warm(3)
         w_mult(1)
         w_tr(1)
+        keep_warm(2)
         t_unit(1)
         a_unit(0, 0, acc[(0, 0)])
         w_q(1)
-        keep_warm(2)
         acc[(0, 1)] = g_unit(0, 1)
         w_mult(2)
         w_tr(2)
@@ -255,15 +270,18 @@ def tile_skeletonlinear_t_kernel(tc, x, weight, mask, bias, out):
         t_banks = [(u, g) for u in range(3, N_UNITS) for g in range(J)]
         done = 0
         for i in range(2, N_UNITS):
-            n = J + (1 if i in LONGER_RUNS else 0)
+            n = J + (1 if i in (3, 4, 5) else 0)
             for u, g in t_banks[done : done + n]:
                 t_bank(u, g)
             done += n
             if i + 1 < N_UNITS:
                 q_unit(i + 1)
-            for j in range(J):
-                a_unit(i, j, g_unit(i, j))
-                if i >= N_UNITS - SPLIT_LAST:
-                    store(i, j * O, (j + 1) * O)
-            if i < N_UNITS - SPLIT_LAST:
+            if i < N_UNITS - 2:
+                for j in range(J):
+                    a_unit(i, j, g_unit(i, j))
                 store(i)
+            else:
+                for t in range(2):
+                    row_tile(i, t, (0, 1))
+                    row_tile(i, t, (2,))
+                    store(i, t, 1)

@@ -50,6 +50,8 @@ def tile_skeletonlinear_t_kernel(tc, x, weight, mask, bias, out):
         wm = {}
         wg = {}
         wc = {}
+        w_codes = {}
+        w_scales = {}
         ws = {}
         grp = {}
         xc = {}
@@ -114,13 +116,16 @@ def tile_skeletonlinear_t_kernel(tc, x, weight, mask, bias, out):
 
         def w_q(j, cs=None):
             for c in cs or NEIGH[j]:
-                codes = const.tile([P, O], U32, name="wc%d%d" % (j, c), align_bytes=64)
-                scales = const.tile([P, O], U8, name="ws%d%d" % (j, c), align_bytes=64)
+                k = j if (0, c) in wg and j < 2 else 0
+                if k == 0:
+                    w_codes[(j, c)] = const.tile([P, 2 * O], U32, name="wc%d%d" % (j, c), align_bytes=64)
+                    w_scales[(j, c)] = const.tile([P, 2 * O], U8, name="ws%d%d" % (j, c), align_bytes=64)
+                codes, scales = w_codes[(j - k, c)], w_scales[(j - k, c)]
+                wc[(j, c)] = codes[:, k * O : (k + 1) * O]
+                ws[(j, c)] = scales[:, k * O : (k + 1) * O]
                 nc.vector.quantize_mx(
-                    out=codes[:].bitcast(FP8X4), scales=scales[:], in_=wg[(j, c)][:]
+                    out=wc[(j, c)].bitcast(FP8X4), scales=ws[(j, c)], in_=wg[(j, c)][:]
                 )
-                wc[(j, c)] = codes
-                ws[(j, c)] = scales
 
         def t_bank(u, g):
             m, a = unit_macro[u]
@@ -153,8 +158,8 @@ def tile_skeletonlinear_t_kernel(tc, x, weight, mask, bias, out):
                         out=bank[:, t * O : (t + 1) * O],
                         lhsT=xc[u][:, s : s + P].bitcast(FP8X4),
                         lhsT_scale=xs[u][:, s : s + P],
-                        rhs=wc[(j, c)][:].bitcast(FP8X4),
-                        rhs_scale=ws[(j, c)][:],
+                        rhs=wc[(j, c)].bitcast(FP8X4),
+                        rhs_scale=ws[(j, c)],
                         start=(c == NEIGH[j][0]),
                         stop=(c == NEIGH[j][-1]),
                     )
@@ -187,18 +192,23 @@ def tile_skeletonlinear_t_kernel(tc, x, weight, mask, bias, out):
             if u not in osb:
                 osb[u] = outs.tile([P, 2 * N], F32, name="osb", tag="osb")
             bank = ops.tile([P, 2 * O], F32, name="ob", tag="ob")
-            for k, j in enumerate(js):
-                for c in NEIGH[j]:
-                    s = (2 * c + t) * P
-                    nc.tensor.matmul_mx(
-                        out=bank[:, k * O : (k + 1) * O],
-                        lhsT=xc[u][:, s : s + P].bitcast(FP8X4),
-                        lhsT_scale=xs[u][:, s : s + P],
-                        rhs=wc[(j, c)][:].bitcast(FP8X4),
-                        rhs_scale=ws[(j, c)][:],
-                        start=(c == NEIGH[j][0]),
-                        stop=(c == NEIGH[j][-1]),
-                    )
+            passes = (
+                [(c, 0, 2 * O, w_codes[(0, c)][:], w_scales[(0, c)][:]) for c in (0, 1)]
+                + [(2, O, 2 * O, wc[(1, 2)], ws[(1, 2)])]
+                if js == (0, 1)
+                else [(c, 0, O, wc[(2, c)], ws[(2, c)]) for c in (1, 2)]
+            )
+            for n, (c, lo, hi, codes, scales) in enumerate(passes):
+                s = (2 * c + t) * P
+                nc.tensor.matmul_mx(
+                    out=bank[:, lo:hi],
+                    lhsT=xc[u][:, s : s + P].bitcast(FP8X4),
+                    lhsT_scale=xs[u][:, s : s + P],
+                    rhs=codes.bitcast(FP8X4),
+                    rhs_scale=scales,
+                    start=(n == 0),
+                    stop=(n == len(passes) - 1),
+                )
             lo, hi = js[0] * O, (js[-1] + 1) * O
             nc.vector.tensor_tensor(
                 out=osb[u][:, t * N + lo : t * N + hi], in0=bank[:, 0 : hi - lo], in1=bias_sb[:, lo:hi], op=ADD
@@ -277,8 +287,9 @@ def tile_skeletonlinear_t_kernel(tc, x, weight, mask, bias, out):
             if i + 1 < N_UNITS:
                 q_unit(i + 1)
             if i < N_UNITS - 2:
-                for j in range(J):
-                    a_unit(i, j, g_unit(i, j))
+                for t in range(2):
+                    row_tile(i, t, (0, 1))
+                a_unit(i, 2, g_unit(i, 2))
                 store(i)
             else:
                 for t in range(2):

from contextlib import ExitStack

import concourse.mybir as mybir
from concourse.masks import make_identity

F32 = mybir.dt.float32
BF16 = mybir.dt.bfloat16
U32 = mybir.dt.uint32
U8 = mybir.dt.uint8
FP8X4 = mybir.dt.float8_e4m3fn_x4
ADD = mybir.AluOpType.add
MULT = mybir.AluOpType.mult

P = 128
B, J, I, O = 4096, 3, 512, 256
K = J * I
N = J * O
NEIGH = [[c for c in (j - 1, j, j + 1) if 0 <= c < J] for j in range(J)]
N_CHUNKS = sum(len(n) for n in NEIGH)
FLOPS = 2 * B * O * I * N_CHUNKS
BYTES = 2 * B * K + 2 * 2 * O * I * N_CHUNKS + 2 * N + 4 * B * N

MACROS = [2, 2, 2, 2, 2, 2, 4, 4, 4, 4, 4]
N_UNITS = B // (2 * P)
OUT_BUFS = 10
XB = 3


def tile_skeletonlinear_t_kernel(tc, x, weight, mask, bias, out):
    nc = tc.nc
    first_unit = [sum(MACROS[:m]) // 2 for m in range(len(MACROS))]
    unit_macro = []
    for m, n in enumerate(MACROS):
        for a in range(n // 2):
            unit_macro.append((m, a))
    assert len(unit_macro) == N_UNITS

    with ExitStack() as ctx:
        const = ctx.enter_context(tc.tile_pool(name="const", bufs=1))
        ring = ctx.enter_context(tc.tile_pool(name="ring", bufs=3))
        xring = ctx.enter_context(tc.tile_pool(name="xring", bufs=XB))
        outs = ctx.enter_context(tc.tile_pool(name="outs", bufs=OUT_BUFS))
        tps = ctx.enter_context(tc.psum_pool(name="tps", bufs=4))
        ops = ctx.enter_context(tc.psum_pool(name="ops", bufs=4))
        ctx.enter_context(tc.manual_schedule())

        x_words = {}
        wt3 = {}
        mk3 = {}
        wm = {}
        wg = {}
        wc = {}
        w_codes = {}
        w_scales = {}
        ws = {}
        grp = {}
        xc = {}
        xs = {}
        osb = {}

        def load_x(m):
            n = MACROS[m]
            r0 = first_unit[m] * 2 * P
            t = const.tile([P, n * K], BF16, name="x%d" % m)
            nc.sync.dma_start(
                out=t[:], in_=x[r0 : r0 + P * n, :].rearrange("(p t) k -> p (t k)", t=n)
            )
            x_words[m] = t[:].bitcast(F32)

        def load_w(j):
            lo = NEIGH[j][0] * I
            hi = (NEIGH[j][-1] + 1) * I
            for views, src, nm in ((wt3, weight, "wt%d"), (mk3, mask, "mk%d")):
                t = outs.tile([P, 2 * (hi - lo)], BF16, name=nm % j, tag="osb")
                view = t[:].rearrange("p (i k) -> p i k", i=2)
                nc.sync.dma_start(
                    out=view,
                    in_=src[j * O : (j + 1) * O, lo:hi].rearrange("(i p) k -> p i k", p=P),
                )
                views[j] = view

        def transposes4(words, cols):
            bank = tps.tile([P, 4 * P], F32, name="tb", tag="tb")
            for k, col in enumerate(cols):
                nc.tensor.transpose(
                    out=bank[:, k * P : (k + 1) * P],
                    in_=words[:, col : col + P],
                    identity=ident[:],
                )
            return bank

        def regroup(bank, dst_words):
            nc.scalar.copy(
                out=dst_words.rearrange("p (q r h) -> p q r h", q=2, h=2),
                in_=bank[:].rearrange("p (q h r) -> p q r h", q=2, h=2),
            )

        def w_mult(j, cs=None):
            for c in cs or NEIGH[j]:
                cl = c - NEIGH[j][0]
                t = ring.tile([P, 2 * I], BF16, name="wm", tag="wm")
                nc.vector.tensor_tensor(
                    out=t[:].rearrange("p (i k) -> p i k", i=2),
                    in0=wt3[j][:, :, cl * I : (cl + 1) * I],
                    in1=mk3[j][:, :, cl * I : (cl + 1) * I],
                    op=MULT,
                )
                wm[(j, c)] = t

        def w_tr(j, cs=None):
            for c in cs or NEIGH[j]:
                bank = transposes4(wm[(j, c)][:].bitcast(F32), [0, P, 2 * P, 3 * P])
                g = ring.tile([P, 4 * O], BF16, name="wg", tag="wg", align_bytes=64)
                regroup(bank, g[:].bitcast(F32))
                wg[(j, c)] = g

        def w_q(j, cs=None):
            for c in cs or NEIGH[j]:
                k = j if (0, c) in wg and j < 2 else 0
                if k == 0:
                    w_codes[(j, c)] = const.tile([P, 2 * O], U32, name="wc%d%d" % (j, c), align_bytes=64)
                    w_scales[(j, c)] = const.tile([P, 2 * O], U8, name="ws%d%d" % (j, c), align_bytes=64)
                codes, scales = w_codes[(j - k, c)], w_scales[(j - k, c)]
                wc[(j, c)] = codes[:, k * O : (k + 1) * O]
                ws[(j, c)] = scales[:, k * O : (k + 1) * O]
                nc.vector.quantize_mx(
                    out=wc[(j, c)].bitcast(FP8X4), scales=ws[(j, c)], in_=wg[(j, c)][:]
                )

        def t_bank(u, g):
            m, a = unit_macro[u]
            if g == 0:
                grp[u] = xring.tile([P, 2 * K], BF16, name="grp", tag="grp", align_bytes=64)
            cols = [a * K + t * (K // 2) + g * (I // 2) + h * P for t in range(2) for h in range(2)]
            bank = transposes4(x_words[m], cols)
            regroup(bank, grp[u][:].bitcast(F32)[:, g * 4 * P : (g + 1) * 4 * P])

        def t_unit(u):
            for g in range(J):
                t_bank(u, g)

        def q_unit(u):
            xc[u] = xring.tile([P, 2 * J * P], U32, name="xc", tag="xc", align_bytes=64)
            xs[u] = xring.tile([P, 2 * J * P], U8, name="xs", tag="xs", align_bytes=64)
            for lo, hi in ((0, 4 * P), (4 * P, 6 * P)):
                nc.vector.quantize_mx(
                    out=xc[u][:, lo:hi].bitcast(FP8X4),
                    scales=xs[u][:, lo:hi],
                    in_=grp[u][:, 4 * lo : 4 * hi],
                )

        def g_unit(u, j):
            bank = ops.tile([P, 2 * O], F32, name="ob", tag="ob")
            for t in range(2):
                for c in NEIGH[j]:
                    s = (2 * c + t) * P
                    nc.tensor.matmul_mx(
                        out=bank[:, t * O : (t + 1) * O],
                        lhsT=xc[u][:, s : s + P].bitcast(FP8X4),
                        lhsT_scale=xs[u][:, s : s + P],
                        rhs=wc[(j, c)].bitcast(FP8X4),
                        rhs_scale=ws[(j, c)],
                        start=(c == NEIGH[j][0]),
                        stop=(c == NEIGH[j][-1]),
                    )
            return bank

        def a_unit(u, j, bank):
            if u not in osb:
                osb[u] = outs.tile([P, 2 * N], F32, name="osb", tag="osb")
            dst = osb[u][:].rearrange("p (t o) -> p t o", t=2)[:, :, j * O : (j + 1) * O]
            acc = bank[:].rearrange("p (t o) -> p t o", t=2)
            bias_j = bias_sb[:, j * O : (j + 1) * O].unsqueeze(1).to_broadcast([P, 2, O])
            nc.vector.tensor_tensor(out=dst, in0=acc, in1=bias_j, op=ADD)

        def store(u, t0=0, n_rows=2):
            m, a = unit_macro[u]
            n = MACROS[m]
            r0 = first_unit[m] * 2 * P
            dram = out[r0 : r0 + P * n, :].rearrange("(p t) o -> p t o", t=n)
            nc.sync.dma_start(
                out=dram[:, 2 * a + t0 : 2 * a + t0 + n_rows, :],
                in_=osb[u][:].rearrange("p (t o) -> p t o", t=2)[:, t0 : t0 + n_rows, :],
            )

        def keep_warm(n):
            bank = ops.tile([P, 2 * O], F32, name="ob", tag="ob")
            for r in range(n):
                nc.tensor.matmul(out=bank[:], lhsT=filler[:, 0:P], rhs=filler[:], start=True, stop=True)

        def row_tile(u, t, js):
            if u not in osb:
                osb[u] = outs.tile([P, 2 * N], F32, name="osb", tag="osb")
            bank = ops.tile([P, 2 * O], F32, name="ob", tag="ob")
            passes = (
                [(c, 0, 2 * O, w_codes[(0, c)][:], w_scales[(0, c)][:]) for c in (0, 1)]
                + [(2, O, 2 * O, wc[(1, 2)], ws[(1, 2)])]
                if js == (0, 1)
                else [(c, 0, O, wc[(2, c)], ws[(2, c)]) for c in (1, 2)]
            )
            for n, (c, lo, hi, codes, scales) in enumerate(passes):
                s = (2 * c + t) * P
                nc.tensor.matmul_mx(
                    out=bank[:, lo:hi],
                    lhsT=xc[u][:, s : s + P].bitcast(FP8X4),
                    lhsT_scale=xs[u][:, s : s + P],
                    rhs=codes.bitcast(FP8X4),
                    rhs_scale=scales,
                    start=(n == 0),
                    stop=(n == len(passes) - 1),
                )
            lo, hi = js[0] * O, (js[-1] + 1) * O
            nc.vector.tensor_tensor(
                out=osb[u][:, t * N + lo : t * N + hi], in0=bank[:, 0 : hi - lo], in1=bias_sb[:, lo:hi], op=ADD
            )

        filler = const.tile([P, 2 * O], BF16, name="filler")
        nc.vector.memset(filler[:], 0.0)
        brow = const.tile([P, N], BF16, name="brow")
        ones = const.tile([P, P], BF16, name="ones")
        ident = const.tile([P, P], F32, name="ident")
        bias_sb = const.tile([P, N], F32, name="bias_sb")
        nc.vector.memset(brow[:], 0.0)
        nc.vector.memset(ones[:], 1.0)
        make_identity(nc, ident[:])

        load_w(0)
        load_x(0)
        nc.sync.dma_start(out=brow[0:1, :], in_=bias.rearrange("(o n) -> o n", o=1))
        load_w(1)
        load_x(1)
        load_w(2)
        for m in range(2, len(MACROS)):
            load_x(m)

        def bias_to_all_partitions():
            for lo, hi in ((0, 512), (512, N)):
                bank = ops.tile([P, 2 * O], F32, name="ob", tag="ob")
                nc.tensor.matmul(
                    out=bank[:, 0 : hi - lo], lhsT=ones[:], rhs=brow[:, lo:hi], start=True, stop=True
                )
                nc.scalar.copy(out=bias_sb[:, lo:hi], in_=bank[:, 0 : hi - lo])

        acc = {}
        keep_warm(11)
        w_mult(0)
        w_tr(0)
        t_unit(0)
        bias_to_all_partitions()
        keep_warm(2)
        w_q(0)
        q_unit(0)
        acc[(0, 0)] = g_unit(0, 0)
        keep_warm(3)
        w_mult(1)
        w_tr(1)
        keep_warm(2)
        t_unit(1)
        a_unit(0, 0, acc[(0, 0)])
        w_q(1)
        acc[(0, 1)] = g_unit(0, 1)
        w_mult(2)
        w_tr(2)
        q_unit(1)
        t_unit(2)
        acc[(1, 0)] = g_unit(1, 0)
        acc[(1, 1)] = g_unit(1, 1)
        a_unit(0, 1, acc[(0, 1)])
        w_q(2)
        a_unit(1, 0, acc[(1, 0)])
        acc[(0, 2)] = g_unit(0, 2)
        acc[(1, 2)] = g_unit(1, 2)
        a_unit(1, 1, acc[(1, 1)])
        q_unit(2)
        a_unit(0, 2, acc[(0, 2)])
        store(0)
        a_unit(1, 2, acc[(1, 2)])
        store(1)

        t_banks = [(u, g) for u in range(3, N_UNITS) for g in range(J)]
        done = 0
        for i in range(2, N_UNITS):
            n = J + (1 if i in (3, 4, 5) else 0)
            for u, g in t_banks[done : done + n]:
                t_bank(u, g)
            done += n
            if i + 1 < N_UNITS:
                q_unit(i + 1)
            if i < N_UNITS - 2:
                for t in range(2):
                    row_tile(i, t, (0, 1))
                a_unit(i, 2, g_unit(i, 2))
                store(i)
            else:
                for t in range(2):
                    row_tile(i, t, (0, 1))
                    row_tile(i, t, (2,))
                    store(i, t, 1)
